import numpy as np
import ml_dtypes


BF16 = ml_dtypes.bfloat16


def bf(x):
    return np.asarray(x, np.float32).astype(BF16)


def f64(x):
    return np.asarray(x).astype(np.float64)


E2M1 = np.array([0.0, 0.5, 1.0, 1.5, 2.0, 3.0, 4.0, 6.0, -0.0, -0.5, -1.0, -1.5, -2.0, -3.0, -4.0, -6.0])


def pack_weight(w, fmt):
    k, n = w.shape
    w = f64(bf(w)).reshape(k // 32, 32, n)
    amax = np.abs(w).max(1)
    if fmt == "e4m3":
        byte = np.frexp(amax)[1] - 1 + 127 - 7
    else:
        mant, ex = np.frexp(amax / 6.0)
        byte = np.where(mant > 0.5, ex, ex - 1) + 127
    byte = np.clip(np.where(amax > 0, byte, 1), 1, 254)
    scaled = (w * np.exp2(127.0 - byte)[:, None, :]).reshape(k, n).astype(np.float32)
    by_word = np.ascontiguousarray(scaled.reshape(k // 512, 128, 4, n).transpose(0, 1, 3, 2))
    if fmt == "e4m3":
        words = by_word.astype(ml_dtypes.float8_e4m3fn).view(np.uint8)
    else:
        c = by_word.astype(ml_dtypes.float4_e2m1fn).view(np.uint8) & 0xF
        words = c[..., 0::2] | (c[..., 1::2] << 4)
    return np.ascontiguousarray(words), np.ascontiguousarray(byte.astype(np.uint8).reshape(k // 512, 16, n))


def unpack_weight(words, scales, fmt):
    g, p, n, _ = words.shape
    if fmt == "e4m3":
        vals = np.ascontiguousarray(words).view(ml_dtypes.float8_e4m3fn).astype(np.float64)
    else:
        nib = np.empty((g, p, n, 4), np.uint8)
        nib[..., 0::2] = words & 0xF
        nib[..., 1::2] = words >> 4
        vals = E2M1[nib]
    vals = vals * np.repeat(np.exp2(scales.astype(np.float64) - 127.0), 8, axis=1)[..., None]
    return vals.transpose(0, 1, 3, 2).reshape(g * 512, n)

def pack4(w):
    words, scales = pack_weight(w, "e2m1")
    return words.reshape(words.shape[0], 128, -1), scales


def unpack4(words, scales):
    return unpack_weight(words.reshape(words.shape[0], 128, -1, 2), scales, "e2m1")


def kspread(k):
    return np.exp2(np.repeat(np.random.randint(-6, 7, k // 32), 32).astype(np.float64))


B, C, K, BK, BN = 512, 4096, 2048, 1, 16
KEEP = 0.3


def setup_inputs():
    s = kspread(C)
    x = np.random.standard_normal((B, C)) * s
    weight = np.random.uniform(-1.0, 1.0, (K, C)) * 3.2 / np.sqrt(C)
    blk = (np.random.uniform(0.0, 1.0, (K // BK, C // BN)) < KEEP).astype(np.float64)
    mask = np.repeat(np.repeat(blk, BK, axis=0), BN, axis=1)
    weight = weight * mask / s[None, :]
    bias = np.random.uniform(-1.0, 1.0, K) * 0.5
    words, scales = pack4(np.ascontiguousarray(weight.T))
    x_words, x_scales = pack4(np.ascontiguousarray(x.T))
    return {"x_words": x_words, "x_scales": x_scales, "weight_words": words, "weight_scales": scales, "bias": bf(bias)}


def reference(x_words, x_scales, weight_words, weight_scales, bias):
    return np.maximum((unpack4(x_words, x_scales).T @ unpack4(weight_words, weight_scales)) + f64(bias), 0.0)

@@ -1,0 +1,184 @@
+from contextlib import ExitStack
+
+import concourse.mybir as mybir
+
+ROWS, K, COLS = 512, 4096, 2048
+FLOPS = 2 * ROWS * K * COLS
+
+F32 = mybir.dt.float32
+BF16 = mybir.dt.bfloat16
+I32 = mybir.dt.int32
+U8 = mybir.dt.uint8
+FP4X4 = mybir.dt.float4_e2m1fn_x4
+ADD = mybir.AluOpType.add
+RELU = mybir.ActivationFunctionType.Relu
+
+P = 128
+G = K // 512
+MT = ROWS // P
+NT = COLS // 512
+WARM = 5
+SWITCH = 6
+
+
+def tile_sparselinearrelu_kernel(tc, x_words, x_scales, weight_words, weight_scales, bias, out):
+    nc = tc.nc
+    with ExitStack() as ctx:
+        keep = ctx.enter_context(tc.tile_pool(name="keep", bufs=1))
+        psum = ctx.enter_context(tc.psum_pool(name="psum", bufs=1))
+        ctx.enter_context(tc.manual_schedule())
+
+        x_code = {}
+        for lo, hi in ((0, 1), (1, 2), (2, 4), (4, 8)):
+            t = keep.tile([P, hi - lo, 2 * ROWS], U8, name=f"x_code_{lo}", align_bytes=256)
+            for g in range(lo, hi):
+                x_code[g] = (t, g - lo)
+        x_plane = keep.tile([P, G, ROWS], U8, name="x_plane", align_bytes=256)
+        w_plane = {}
+        w_plane_tile = {}
+        for half, lo, hi in ((0, 0, 2), (0, 2, 5), (0, 5, 8), (1, 0, 8)):
+            t = keep.tile([P, hi - lo, COLS // 2], U8, name=f"w_plane_{half}_{lo}", align_bytes=256)
+            w_plane_tile[half, lo] = t
+            for g in range(lo, hi):
+                w_plane[half, g] = (t, g - lo)
+        w_code = {}
+        w_00 = []
+        for nb in range(2):
+            t = keep.tile([P, 1024], U8, name=f"w_code_00_{nb}", align_bytes=256)
+            w_00.append(t)
+            w_code[0, nb] = t[:, :]
+        w_half = {}
+        for half in range(2):
+            for g in range(G):
+                if (half, g) == (0, 0):
+                    continue
+                t = keep.tile([P, 2048], U8, name=f"w_code_{half}_{g}", align_bytes=256)
+                w_half[half, g] = t
+                for j in range(2):
+                    w_code[g, 2 * half + j] = t[:, 1024 * j : 1024 * (j + 1)]
+        warm = keep.tile([P, 512], BF16, name="warm")
+        bias_rows = keep.tile([P, 512], BF16, name="bias_rows")
+        pick = keep.tile([P, NT], BF16, name="pick")
+        bias_sb = [keep.tile([P, 512], F32, name=f"bias_sb_{nb}") for nb in range(NT)]
+
+        def load_x(lo, hi):
+            t = x_code[lo][0]
+            nc.sync.dma_start(
+                out=t[:, :, :].bitcast(I32), in_=x_words[lo:hi, :, :].rearrange("g p c -> p g c").bitcast(I32)
+            )
+
+        def load_w(half, g):
+            nc.sync.dma_start(
+                out=w_half[half, g][:, :].bitcast(I32),
+                in_=weight_words[g, :, 2048 * half : 2048 * (half + 1)].bitcast(I32),
+            )
+
+        def load_w00(nb):
+            nc.sync.dma_start(
+                out=w_00[nb][:, :].bitcast(I32), in_=weight_words[0, :, 1024 * nb : 1024 * (nb + 1)].bitcast(I32)
+            )
+
+        def load_scales(t, source):
+            for q in range(4):
+                nc.sync.dma_start(
+                    out=t[32 * q : 32 * q + 4, :, :].bitcast(I32),
+                    in_=source[:, 4 * q : 4 * q + 4, :].rearrange("g r n -> r g n").bitcast(I32),
+                )
+
+        def load_ws(half, lo, hi):
+            load_scales(
+                w_plane_tile[half, lo], weight_scales[lo:hi, :, 1024 * half : 1024 * (half + 1)]
+            )
+
+        nc.vector.memset(x_plane[:, :, :].bitcast(I32), 0)
+        nc.vector.memset(w_plane_tile[0, 0][:, :, :].bitcast(I32), 0)
+        nc.gpsimd.memset(warm[:, :], 0.0)
+        nc.gpsimd.memset(bias_rows[:, :], 0.0)
+        nc.gpsimd.dma_start(out=bias_rows[0:P:32, :], in_=bias.rearrange("(j n) -> j n", n=512))
+        nc.gpsimd.memset(pick[:, :], 0.0)
+        for j in range(NT):
+            nc.gpsimd.memset(pick[32 * j : 32 * j + 1, j : j + 1], 1.0)
+        nc.vector.memset(w_plane_tile[0, 2][:, :, :].bitcast(I32), 0)
+        nc.vector.memset(w_plane_tile[0, 5][:, :, :].bitcast(I32), 0)
+        nc.vector.memset(w_plane_tile[1, 0][:, :, :].bitcast(I32), 0)
+
+        load_x(0, 1)
+        load_w00(0)
+        load_scales(x_plane, x_scales)
+        load_ws(0, 0, 2)
+        load_w00(1)
+        load_x(1, 2)
+        load_w(0, 1)
+        load_ws(0, 2, 5)
+        load_x(2, 4)
+        load_w(0, 2)
+        load_w(0, 3)
+        load_x(4, 8)
+        load_w(0, 4)
+        load_ws(0, 5, 8)
+        load_w(0, 5)
+        load_w(0, 6)
+        load_w(0, 7)
+        load_ws(1, 0, 8)
+        for g in range(G):
+            load_w(1, g)
+
+        junk = psum.tile([P, 512], F32, name="junk", tag="bank3")
+        for i in range(WARM):
+            nc.tensor.matmul(junk[:, :], lhsT=warm[:, 0:P], rhs=warm[:, :], start=True, stop=True)
+        for nb in range(NT):
+            spread = psum.tile([P, 512], F32, name=f"spread_{nb}", tag=f"bank{4 + nb}")
+            nc.tensor.matmul(
+                spread[:, :], lhsT=pick[:, nb : nb + 1].to_broadcast([P, P]), rhs=bias_rows[:, :], start=True, stop=True
+            )
+            nc.scalar.copy(bias_sb[nb][:, :], spread[:, :])
+
+        def mx(acc, m, nb, g, cols=slice(0, 512)):
+            xt, xi = x_code[g]
+            wt, wi = w_plane[nb // 2, g]
+            c0 = 512 * (nb % 2)
+            nc.tensor.matmul_mx(
+                out=acc[:, :],
+                lhsT=xt[:, xi, 256 * m : 256 * (m + 1)].bitcast(FP4X4),
+                lhsT_scale=x_plane[:, g, P * m : P * (m + 1)],
+                rhs=w_code[g, nb][:, 2 * cols.start : 2 * cols.stop].bitcast(FP4X4),
+                rhs_scale=wt[:, wi, c0 + cols.start : c0 + cols.stop],
+                start=(g == 0),
+                stop=(g == G - 1),
+            )
+
+        def finish(acc, m, nb, cols=slice(0, 512), last=False):
+            width = cols.stop - cols.start
+            o = keep.tile([P, width], F32, name=f"o_{m}_{nb}_{cols.start}")
+            nc.vector.tensor_tensor(out=o[:, :], in0=acc[:, :], in1=bias_sb[nb][:, cols], op=ADD)
+            if last:
+                nc.vector.tensor_scalar_max(o[:, :], o[:, :], 0.0)
+            else:
+                nc.scalar.activation(o[:, :], o[:, :], RELU)
+            nc.sync.dma_start(
+                out=out[P * m : P * (m + 1), 512 * nb + cols.start : 512 * nb + cols.stop], in_=o[:, :]
+            )
+
+        sweep = [(m, nb) for nb in range(2) for m in range(MT)]
+        accs = [psum.tile([P, 512], F32, name=f"acc_0_{i}", tag=f"bank{i}") for i in range(8)]
+        for g in range(SWITCH):
+            for i, (m, nb) in enumerate(sweep):
+                mx(accs[i], m, nb, g)
+        for i, (m, nb) in enumerate(sweep):
+            for g in range(SWITCH, G):
+                mx(accs[i], m, nb, g)
+            finish(accs[i], m, nb)
+
+        for i, (m, nb) in enumerate([(m, nb) for nb in range(2, 4) for m in range(MT)]):
+            if i < 7:
+                acc = psum.tile([P, 512], F32, name=f"acc_1_{i}", tag=f"bank{i}")
+                for g in range(G):
+                    mx(acc, m, nb, g)
+                finish(acc, m, nb)
+            else:
+                for j in range(2):
+                    cols = slice(256 * j, 256 * (j + 1))
+                    acc = psum.tile([P, 256], F32, name=f"acc_last_{j}", tag=("bank7", "bank0")[j])
+                    for g in range(G):
+                        mx(acc, m, nb, g, cols)
+                    finish(acc, m, nb, cols, last=True)

@@ -17,7 +17,7 @@ P = 128
 G = K // 512
 MT = ROWS // P
 NT = COLS // 512
-WARM = 5
+WARM = 4
 SWITCH = 6
 
 
@@ -33,7 +33,13 @@ def tile_sparselinearrelu_kernel(tc, x_words, x_scales, weight_words, weight_sca
             t = keep.tile([P, hi - lo, 2 * ROWS], U8, name=f"x_code_{lo}", align_bytes=256)
             for g in range(lo, hi):
                 x_code[g] = (t, g - lo)
-        x_plane = keep.tile([P, G, ROWS], U8, name="x_plane", align_bytes=256)
+        x_plane = {}
+        x_plane_tile = {}
+        for lo, hi in ((0, 4), (4, 8)):
+            t = keep.tile([P, hi - lo, ROWS], U8, name=f"x_plane_{lo}", align_bytes=256)
+            x_plane_tile[lo] = t
+            for g in range(lo, hi):
+                x_plane[g] = (t, g - lo)
         w_plane = {}
         w_plane_tile = {}
         for half, lo, hi in ((0, 0, 2), (0, 2, 5), (0, 5, 8), (1, 0, 8)):
@@ -90,21 +96,22 @@ def tile_sparselinearrelu_kernel(tc, x_words, x_scales, weight_words, weight_sca
                 w_plane_tile[half, lo], weight_scales[lo:hi, :, 1024 * half : 1024 * (half + 1)]
             )
 
-        nc.vector.memset(x_plane[:, :, :].bitcast(I32), 0)
+        nc.vector.memset(x_plane_tile[0][:, :, :].bitcast(I32), 0)
         nc.vector.memset(w_plane_tile[0, 0][:, :, :].bitcast(I32), 0)
-        nc.gpsimd.memset(warm[:, :], 0.0)
         nc.gpsimd.memset(bias_rows[:, :], 0.0)
-        nc.gpsimd.dma_start(out=bias_rows[0:P:32, :], in_=bias.rearrange("(j n) -> j n", n=512))
+        nc.gpsimd.memset(warm[:, :], 0.0)
         nc.gpsimd.memset(pick[:, :], 0.0)
         for j in range(NT):
             nc.gpsimd.memset(pick[32 * j : 32 * j + 1, j : j + 1], 1.0)
         nc.vector.memset(w_plane_tile[0, 2][:, :, :].bitcast(I32), 0)
+        nc.vector.memset(x_plane_tile[4][:, :, :].bitcast(I32), 0)
         nc.vector.memset(w_plane_tile[0, 5][:, :, :].bitcast(I32), 0)
         nc.vector.memset(w_plane_tile[1, 0][:, :, :].bitcast(I32), 0)
 
         load_x(0, 1)
         load_w00(0)
-        load_scales(x_plane, x_scales)
+        nc.scalar.dma_start(out=bias_rows[0:P:32, :], in_=bias.rearrange("(j n) -> j n", n=512))
+        load_scales(x_plane_tile[0], x_scales[0:4, :, :])
         load_ws(0, 0, 2)
         load_w00(1)
         load_x(1, 2)
@@ -115,6 +122,7 @@ def tile_sparselinearrelu_kernel(tc, x_words, x_scales, weight_words, weight_sca
         load_w(0, 3)
         load_x(4, 8)
         load_w(0, 4)
+        load_scales(x_plane_tile[4], x_scales[4:8, :, :])
         load_ws(0, 5, 8)
         load_w(0, 5)
         load_w(0, 6)
@@ -133,14 +141,16 @@ def tile_sparselinearrelu_kernel(tc, x_words, x_scales, weight_words, weight_sca
             )
             nc.scalar.copy(bias_sb[nb][:, :], spread[:, :])
 
+
         def mx(acc, m, nb, g, cols=slice(0, 512)):
             xt, xi = x_code[g]
+            xp, pi = x_plane[g]
             wt, wi = w_plane[nb // 2, g]
             c0 = 512 * (nb % 2)
             nc.tensor.matmul_mx(
                 out=acc[:, :],
                 lhsT=xt[:, xi, 256 * m : 256 * (m + 1)].bitcast(FP4X4),
-                lhsT_scale=x_plane[:, g, P * m : P * (m + 1)],
+                lhsT_scale=xp[:, pi, P * m : P * (m + 1)],
                 rhs=w_code[g, nb][:, 2 * cols.start : 2 * cols.stop].bitcast(FP4X4),
                 rhs_scale=wt[:, wi, c0 + cols.start : c0 + cols.stop],
                 start=(g == 0),
@@ -176,9 +186,9 @@ def tile_sparselinearrelu_kernel(tc, x_words, x_scales, weight_words, weight_sca
                     mx(acc, m, nb, g)
                 finish(acc, m, nb)
             else:
-                for j in range(2):
-                    cols = slice(256 * j, 256 * (j + 1))
-                    acc = psum.tile([P, 256], F32, name=f"acc_last_{j}", tag=("bank7", "bank0")[j])
+                for j, (c0, c1) in enumerate(((0, 256), (256, 384), (384, 512))):
+                    cols = slice(c0, c1)
+                    acc = psum.tile([P, c1 - c0], F32, name=f"acc_last_{j}", tag=("bank7", "bank0", "bank1")[j])
                     for g in range(G):
                         mx(acc, m, nb, g, cols)
                     finish(acc, m, nb, cols, last=True)

@@ -17,7 +17,7 @@ P = 128
 G = K // 512
 MT = ROWS // P
 NT = COLS // 512
-WARM = 4
+WARM = 5
 SWITCH = 6
 
 
@@ -35,7 +35,7 @@ def tile_sparselinearrelu_kernel(tc, x_words, x_scales, weight_words, weight_sca
                 x_code[g] = (t, g - lo)
         x_plane = {}
         x_plane_tile = {}
-        for lo, hi in ((0, 4), (4, 8)):
+        for lo, hi in ((0, 3), (3, 8)):
             t = keep.tile([P, hi - lo, ROWS], U8, name=f"x_plane_{lo}", align_bytes=256)
             x_plane_tile[lo] = t
             for g in range(lo, hi):
@@ -96,33 +96,33 @@ def tile_sparselinearrelu_kernel(tc, x_words, x_scales, weight_words, weight_sca
                 w_plane_tile[half, lo], weight_scales[lo:hi, :, 1024 * half : 1024 * (half + 1)]
             )
 
-        nc.vector.memset(x_plane_tile[0][:, :, :].bitcast(I32), 0)
+        nc.vector.memset(warm[:, :].bitcast(I32), 0)
         nc.vector.memset(w_plane_tile[0, 0][:, :, :].bitcast(I32), 0)
-        nc.gpsimd.memset(bias_rows[:, :], 0.0)
-        nc.gpsimd.memset(warm[:, :], 0.0)
+        nc.vector.memset(x_plane_tile[0][:, :, :].bitcast(I32), 0)
+        nc.gpsimd.memset(bias_rows[:, :].bitcast(I32), 0)
         nc.gpsimd.memset(pick[:, :], 0.0)
         for j in range(NT):
             nc.gpsimd.memset(pick[32 * j : 32 * j + 1, j : j + 1], 1.0)
         nc.vector.memset(w_plane_tile[0, 2][:, :, :].bitcast(I32), 0)
-        nc.vector.memset(x_plane_tile[4][:, :, :].bitcast(I32), 0)
+        nc.vector.memset(x_plane_tile[3][:, :, :].bitcast(I32), 0)
         nc.vector.memset(w_plane_tile[0, 5][:, :, :].bitcast(I32), 0)
         nc.vector.memset(w_plane_tile[1, 0][:, :, :].bitcast(I32), 0)
 
+        nc.scalar.dma_start(out=bias_rows[0:P:32, :], in_=bias.rearrange("(j n) -> j n", n=512))
         load_x(0, 1)
         load_w00(0)
-        nc.scalar.dma_start(out=bias_rows[0:P:32, :], in_=bias.rearrange("(j n) -> j n", n=512))
-        load_scales(x_plane_tile[0], x_scales[0:4, :, :])
         load_ws(0, 0, 2)
+        load_scales(x_plane_tile[0], x_scales[0:3, :, :])
         load_w00(1)
         load_x(1, 2)
         load_w(0, 1)
-        load_ws(0, 2, 5)
         load_x(2, 4)
         load_w(0, 2)
+        load_ws(0, 2, 5)
         load_w(0, 3)
+        load_scales(x_plane_tile[3], x_scales[3:8, :, :])
         load_x(4, 8)
         load_w(0, 4)
-        load_scales(x_plane_tile[4], x_scales[4:8, :, :])
         load_ws(0, 5, 8)
         load_w(0, 5)
         load_w(0, 6)

from contextlib import ExitStack

import concourse.mybir as mybir

ROWS, K, COLS = 512, 4096, 2048
FLOPS = 2 * ROWS * K * COLS

F32 = mybir.dt.float32
BF16 = mybir.dt.bfloat16
I32 = mybir.dt.int32
U8 = mybir.dt.uint8
FP4X4 = mybir.dt.float4_e2m1fn_x4
ADD = mybir.AluOpType.add
RELU = mybir.ActivationFunctionType.Relu

P = 128
G = K // 512
MT = ROWS // P
NT = COLS // 512
WARM = 5
SWITCH = 6


def tile_sparselinearrelu_kernel(tc, x_words, x_scales, weight_words, weight_scales, bias, out):
    nc = tc.nc
    with ExitStack() as ctx:
        keep = ctx.enter_context(tc.tile_pool(name="keep", bufs=1))
        psum = ctx.enter_context(tc.psum_pool(name="psum", bufs=1))
        ctx.enter_context(tc.manual_schedule())

        x_code = {}
        for lo, hi in ((0, 1), (1, 2), (2, 4), (4, 8)):
            t = keep.tile([P, hi - lo, 2 * ROWS], U8, name=f"x_code_{lo}", align_bytes=256)
            for g in range(lo, hi):
                x_code[g] = (t, g - lo)
        x_plane = {}
        x_plane_tile = {}
        for lo, hi in ((0, 3), (3, 8)):
            t = keep.tile([P, hi - lo, ROWS], U8, name=f"x_plane_{lo}", align_bytes=256)
            x_plane_tile[lo] = t
            for g in range(lo, hi):
                x_plane[g] = (t, g - lo)
        w_plane = {}
        w_plane_tile = {}
        for half, lo, hi in ((0, 0, 2), (0, 2, 5), (0, 5, 8), (1, 0, 8)):
            t = keep.tile([P, hi - lo, COLS // 2], U8, name=f"w_plane_{half}_{lo}", align_bytes=256)
            w_plane_tile[half, lo] = t
            for g in range(lo, hi):
                w_plane[half, g] = (t, g - lo)
        w_code = {}
        w_00 = []
        for nb in range(2):
            t = keep.tile([P, 1024], U8, name=f"w_code_00_{nb}", align_bytes=256)
            w_00.append(t)
            w_code[0, nb] = t[:, :]
        w_half = {}
        for half in range(2):
            for g in range(G):
                if (half, g) == (0, 0):
                    continue
                t = keep.tile([P, 2048], U8, name=f"w_code_{half}_{g}", align_bytes=256)
                w_half[half, g] = t
                for j in range(2):
                    w_code[g, 2 * half + j] = t[:, 1024 * j : 1024 * (j + 1)]
        warm = keep.tile([P, 512], BF16, name="warm")
        bias_rows = keep.tile([P, 512], BF16, name="bias_rows")
        pick = keep.tile([P, NT], BF16, name="pick")
        bias_sb = [keep.tile([P, 512], F32, name=f"bias_sb_{nb}") for nb in range(NT)]

        def load_x(lo, hi):
            t = x_code[lo][0]
            nc.sync.dma_start(
                out=t[:, :, :].bitcast(I32), in_=x_words[lo:hi, :, :].rearrange("g p c -> p g c").bitcast(I32)
            )

        def load_w(half, g):
            nc.sync.dma_start(
                out=w_half[half, g][:, :].bitcast(I32),
                in_=weight_words[g, :, 2048 * half : 2048 * (half + 1)].bitcast(I32),
            )

        def load_w00(nb):
            nc.sync.dma_start(
                out=w_00[nb][:, :].bitcast(I32), in_=weight_words[0, :, 1024 * nb : 1024 * (nb + 1)].bitcast(I32)
            )

        def load_scales(t, source):
            for q in range(4):
                nc.sync.dma_start(
                    out=t[32 * q : 32 * q + 4, :, :].bitcast(I32),
                    in_=source[:, 4 * q : 4 * q + 4, :].rearrange("g r n -> r g n").bitcast(I32),
                )

        def load_ws(half, lo, hi):
            load_scales(
                w_plane_tile[half, lo], weight_scales[lo:hi, :, 1024 * half : 1024 * (half + 1)]
            )

        nc.vector.memset(warm[:, :].bitcast(I32), 0)
        nc.vector.memset(w_plane_tile[0, 0][:, :, :].bitcast(I32), 0)
        nc.vector.memset(x_plane_tile[0][:, :, :].bitcast(I32), 0)
        nc.gpsimd.memset(bias_rows[:, :].bitcast(I32), 0)
        nc.gpsimd.memset(pick[:, :], 0.0)
        for j in range(NT):
            nc.gpsimd.memset(pick[32 * j : 32 * j + 1, j : j + 1], 1.0)
        nc.vector.memset(w_plane_tile[0, 2][:, :, :].bitcast(I32), 0)
        nc.vector.memset(x_plane_tile[3][:, :, :].bitcast(I32), 0)
        nc.vector.memset(w_plane_tile[0, 5][:, :, :].bitcast(I32), 0)
        nc.vector.memset(w_plane_tile[1, 0][:, :, :].bitcast(I32), 0)

        nc.scalar.dma_start(out=bias_rows[0:P:32, :], in_=bias.rearrange("(j n) -> j n", n=512))
        load_x(0, 1)
        load_w00(0)
        load_ws(0, 0, 2)
        load_scales(x_plane_tile[0], x_scales[0:3, :, :])
        load_w00(1)
        load_x(1, 2)
        load_w(0, 1)
        load_x(2, 4)
        load_w(0, 2)
        load_ws(0, 2, 5)
        load_w(0, 3)
        load_scales(x_plane_tile[3], x_scales[3:8, :, :])
        load_x(4, 8)
        load_w(0, 4)
        load_ws(0, 5, 8)
        load_w(0, 5)
        load_w(0, 6)
        load_w(0, 7)
        load_ws(1, 0, 8)
        for g in range(G):
            load_w(1, g)

        junk = psum.tile([P, 512], F32, name="junk", tag="bank3")
        for i in range(WARM):
            nc.tensor.matmul(junk[:, :], lhsT=warm[:, 0:P], rhs=warm[:, :], start=True, stop=True)
        for nb in range(NT):
            spread = psum.tile([P, 512], F32, name=f"spread_{nb}", tag=f"bank{4 + nb}")
            nc.tensor.matmul(
                spread[:, :], lhsT=pick[:, nb : nb + 1].to_broadcast([P, P]), rhs=bias_rows[:, :], start=True, stop=True
            )
            nc.scalar.copy(bias_sb[nb][:, :], spread[:, :])


        def mx(acc, m, nb, g, cols=slice(0, 512)):
            xt, xi = x_code[g]
            xp, pi = x_plane[g]
            wt, wi = w_plane[nb // 2, g]
            c0 = 512 * (nb % 2)
            nc.tensor.matmul_mx(
                out=acc[:, :],
                lhsT=xt[:, xi, 256 * m : 256 * (m + 1)].bitcast(FP4X4),
                lhsT_scale=xp[:, pi, P * m : P * (m + 1)],
                rhs=w_code[g, nb][:, 2 * cols.start : 2 * cols.stop].bitcast(FP4X4),
                rhs_scale=wt[:, wi, c0 + cols.start : c0 + cols.stop],
                start=(g == 0),
                stop=(g == G - 1),
            )

        def finish(acc, m, nb, cols=slice(0, 512), last=False):
            width = cols.stop - cols.start
            o = keep.tile([P, width], F32, name=f"o_{m}_{nb}_{cols.start}")
            nc.vector.tensor_tensor(out=o[:, :], in0=acc[:, :], in1=bias_sb[nb][:, cols], op=ADD)
            if last:
                nc.vector.tensor_scalar_max(o[:, :], o[:, :], 0.0)
            else:
                nc.scalar.activation(o[:, :], o[:, :], RELU)
            nc.sync.dma_start(
                out=out[P * m : P * (m + 1), 512 * nb + cols.start : 512 * nb + cols.stop], in_=o[:, :]
            )

        sweep = [(m, nb) for nb in range(2) for m in range(MT)]
        accs = [psum.tile([P, 512], F32, name=f"acc_0_{i}", tag=f"bank{i}") for i in range(8)]
        for g in range(SWITCH):
            for i, (m, nb) in enumerate(sweep):
                mx(accs[i], m, nb, g)
        for i, (m, nb) in enumerate(sweep):
            for g in range(SWITCH, G):
                mx(accs[i], m, nb, g)
            finish(accs[i], m, nb)

        for i, (m, nb) in enumerate([(m, nb) for nb in range(2, 4) for m in range(MT)]):
            if i < 7:
                acc = psum.tile([P, 512], F32, name=f"acc_1_{i}", tag=f"bank{i}")
                for g in range(G):
                    mx(acc, m, nb, g)
                finish(acc, m, nb)
            else:
                for j, (c0, c1) in enumerate(((0, 256), (256, 384), (384, 512))):
                    cols = slice(c0, c1)
                    acc = psum.tile([P, c1 - c0], F32, name=f"acc_last_{j}", tag=("bank7", "bank0", "bank1")[j])
                    for g in range(G):
                        mx(acc, m, nb, g, cols)
                    finish(acc, m, nb, cols, last=True)
